import numpy as np
import ml_dtypes


def mxq(x, axis, fmt="e4m3"):
    dtype, down = {"e4m3": (ml_dtypes.float8_e4m3fn, 7), "e5m2": (ml_dtypes.float8_e5m2, 14)}[fmt]
    v = np.moveaxis(np.asarray(x, np.float32).astype(ml_dtypes.bfloat16).astype(np.float64), axis, -1)
    blocks = v.reshape(v.shape[:-1] + (-1, 32))
    amax = np.abs(blocks).max(-1, keepdims=True)
    byte = np.maximum(np.where(amax > 0, np.frexp(amax)[1] - 1 + 127, 0) - down, 1)
    scale = np.exp2(byte - 127.0)
    codes = (blocks / scale).astype(np.float32).astype(dtype).astype(np.float64)
    return np.moveaxis((codes * scale).reshape(v.shape), -1, axis)


WIDE = False


def mx_kscale(k):
    if not WIDE:
        return np.ones(k)
    levels = np.array([10, -10, 5, -5, 0])
    a = np.random.permutation(np.resize(levels, k // 512 * 4)).reshape(k // 512, 4)
    idx = np.arange(k)
    return np.exp2(a[idx // 512, idx % 128 // 32])


BF16 = ml_dtypes.bfloat16


def bf(x):
    return np.asarray(x, np.float32).astype(BF16)


def f64(x):
    return np.asarray(x).astype(np.float64)


B, T, S, Dt, Df = 2, 512, 512, 2048, 2048
EPS = 1e-6


def rmsnorm(x, w):
    return x * (1.0 / np.sqrt(np.mean(x * x, axis=-1, keepdims=True) + EPS)) * w


def setup_inputs():
    s = mx_kscale(Df)
    return {"features": bf(np.random.standard_normal((B, S, Df))),
            "fn_w": bf((1.0 + 0.1 * np.random.standard_normal(Df)) * s),
            "Wk_w": bf(np.random.standard_normal((Df, Df)) / np.sqrt(Df) / s[None, :]),
            "Wk_b": bf(np.random.standard_normal(Df) * 0.3),
            "kn_w": bf(1.0 + 0.1 * np.random.standard_normal(Df))}


def reference(features, fn_w, Wk_w, Wk_b, kn_w):
    features_n = rmsnorm(f64(features), f64(fn_w))
    k = (mxq(features_n, 2, "e4m3") @ mxq(f64(Wk_w), 1, "e4m3").T) + f64(Wk_b)
    return rmsnorm(k, f64(kn_w))

@@ -1,0 +1,192 @@
+from contextlib import ExitStack
+
+import concourse.mybir as mybir
+from concourse.masks import make_identity
+
+F32 = mybir.dt.float32
+BF16 = mybir.dt.bfloat16
+U32 = mybir.dt.uint32
+U8 = mybir.dt.uint8
+FP8X4 = mybir.dt.float8_e4m3fn_x4
+ALU = mybir.AluOpType
+ACT = mybir.ActivationFunctionType
+
+P = 128
+TOKENS = 1024
+D = 2048
+EPS = 1e-6
+PACK = 4
+K_PASS = P * PACK
+PASSES = D // K_PASS
+WORDS = D // 2
+CHUNK = 512
+CHUNKS = D // CHUNK
+W_TILES_PER_CHUNK = CHUNK // P
+TOKEN_TILES = TOKENS // P
+EARLY = 4
+assert TOKEN_TILES - EARLY == CHUNKS
+
+FLOPS = 2 * TOKENS * D * D
+
+
+def tile_crossattention_pa_kernel(tc, features, fn_w, Wk_w, Wk_b, kn_w, out):
+    nc = tc.nc
+    x_rows = features.flatten_outer_dims()
+    out_rows = out.flatten_outer_dims()
+
+    with ExitStack() as ctx:
+        const = ctx.enter_context(tc.tile_pool(name="const", bufs=1))
+        keep = ctx.enter_context(tc.tile_pool(name="keep", bufs=1))
+        x_in = ctx.enter_context(tc.tile_pool(name="x_in", bufs=4))
+        w_in = ctx.enter_context(tc.tile_pool(name="w_in", bufs=6))
+        work = ctx.enter_context(tc.tile_pool(name="work", bufs=2))
+        k_pool = ctx.enter_context(tc.tile_pool(name="k_pool", bufs=EARLY + 2))
+        psum_t = ctx.enter_context(tc.psum_pool(name="psum_t", bufs=4))
+        psum_mx = ctx.enter_context(tc.psum_pool(name="psum_mx", bufs=4))
+
+        eps = const.tile([P, 1], F32)
+        nc.vector.memset(eps[:], EPS)
+        warm = const.tile([P, 1], F32)
+        nc.scalar.activation(out=warm[:], in_=eps[:], func=ACT.Abs_reciprocal_sqrt)
+        ident = const.tile([P, P], F32)
+        make_identity(nc, ident[:])
+        fn_bc = const.tile([P, D], BF16)
+        bias_bc = const.tile([P, D], BF16)
+        kn_bc = const.tile([P, D], BF16)
+
+        x_codes = keep.tile([P, TOKEN_TILES, PASSES * P], U32, align_bytes=64)
+        x_scales = keep.tile([P, TOKEN_TILES, PASSES * P], U8, align_bytes=64)
+        w_codes = keep.tile([P, CHUNKS, PASSES * CHUNK], U32, align_bytes=64)
+        w_scales = keep.tile([P, CHUNKS, PASSES * CHUNK], U8, align_bytes=64)
+        x_sumsq = keep.tile([P, TOKEN_TILES], F32)
+        x_rstd = keep.tile([P, TOKEN_TILES], F32)
+        k_sumsq_parts = keep.tile([P, TOKEN_TILES, CHUNKS], F32)
+        k_sumsq = keep.tile([P, TOKEN_TILES], F32)
+        k_rstd = keep.tile([P, TOKEN_TILES], F32)
+        x_raw = {}
+        k_tiles = {}
+
+        def load_tokens(i):
+            x_raw[i] = x_in.tile([P, D], BF16, name="x_raw")
+            nc.sync.dma_start(out=x_raw[i][:], in_=x_rows[i * P : (i + 1) * P, :])
+
+        def k_onto_partitions(rows_words, grouped_words, copy):
+            for half in range(2):
+                bank = psum_t.tile([P, 2, 2, P], F32)
+                for c2 in range(2):
+                    for u in range(2):
+                        first = ((2 * half + c2) * 2 + u) * P
+                        nc.tensor.transpose(bank[:, c2, u, :], rows_words[:, first : first + P], ident[:])
+                copy(
+                    out=grouped_words[:, 2 * half : 2 * half + 2, :, :],
+                    in_=bank[:].rearrange("p c u r -> p c r u"),
+                )
+
+        def prepare_tokens(i):
+            squares = work.tile([P, D], BF16)
+            nc.scalar.activation(
+                out=squares[:], in_=x_raw[i][:], func=ACT.Square, accum_out=x_sumsq[:, i : i + 1]
+            )
+            nc.scalar.activation(
+                out=x_rstd[:, i : i + 1],
+                in_=x_sumsq[:, i : i + 1],
+                func=ACT.Abs_reciprocal_sqrt,
+                scale=1.0 / D,
+                bias=eps[:],
+            )
+            x_n = work.tile([P, D], BF16)
+            nc.vector.scalar_tensor_tensor(
+                out=x_n[:], in0=x_raw[i][:], scalar=x_rstd[:, i : i + 1], in1=fn_bc[:], op0=ALU.mult, op1=ALU.mult
+            )
+            x_grouped = work.tile([P, D], BF16, align_bytes=64)
+            k_onto_partitions(
+                x_n[:].bitcast(F32),
+                x_grouped[:].bitcast(F32).rearrange("p (c r u) -> p c r u", c=PASSES, r=P, u=2),
+                nc.vector.tensor_copy if i < EARLY else nc.scalar.copy,
+            )
+            nc.vector.quantize_mx(out=x_codes[:, i, :].bitcast(FP8X4), scales=x_scales[:, i, :], in_=x_grouped[:])
+
+        def prepare_chunk(j):
+            w_grouped = work.tile([P, PASSES * CHUNK * PACK], BF16, align_bytes=64)
+            grouped_words = w_grouped[:].bitcast(F32).rearrange(
+                "p (c n r u) -> p c n r u", c=PASSES, n=W_TILES_PER_CHUNK, r=P, u=2
+            )
+            for n in range(W_TILES_PER_CHUNK):
+                first_row = j * CHUNK + n * P
+                w_raw = w_in.tile([P, D], BF16)
+                nc.sync.dma_start(out=w_raw[:], in_=Wk_w[first_row : first_row + P, :])
+                k_onto_partitions(w_raw[:].bitcast(F32), grouped_words[:, :, n, :, :], nc.scalar.copy)
+            for c in range(PASSES):
+                nc.vector.quantize_mx(
+                    out=w_codes[:, j, c * CHUNK : (c + 1) * CHUNK].bitcast(FP8X4),
+                    scales=w_scales[:, j, c * CHUNK : (c + 1) * CHUNK],
+                    in_=w_grouped[:, c * CHUNK * PACK : (c + 1) * CHUNK * PACK],
+                )
+
+        def multiply(i, j):
+            if j == 0:
+                k_tiles[i] = k_pool.tile([P, D], F32, name="k_tile")
+            acc = psum_mx.tile([P, CHUNK], F32)
+            for c in range(PASSES):
+                nc.tensor.matmul_mx(
+                    out=acc[:],
+                    lhsT=x_codes[:, i, c * P : (c + 1) * P].bitcast(FP8X4),
+                    lhsT_scale=x_scales[:, i, c * P : (c + 1) * P],
+                    rhs=w_codes[:, j, c * CHUNK : (c + 1) * CHUNK].bitcast(FP8X4),
+                    rhs_scale=w_scales[:, j, c * CHUNK : (c + 1) * CHUNK],
+                    start=(c == 0),
+                    stop=(c == PASSES - 1),
+                )
+            cols = slice(j * CHUNK, (j + 1) * CHUNK)
+            nc.vector.tensor_tensor(out=k_tiles[i][:, cols], in0=acc[:], in1=bias_bc[:, cols], op=ALU.add)
+
+        def finish(i):
+            k_tile = k_tiles[i]
+            for j in range(CHUNKS):
+                k_squares = work.tile([P, CHUNK], BF16)
+                nc.scalar.activation(
+                    out=k_squares[:],
+                    in_=k_tile[:, j * CHUNK : (j + 1) * CHUNK],
+                    func=ACT.Square,
+                    accum_out=k_sumsq_parts[:, i, j : j + 1],
+                )
+            parts_copy = work.tile([P, CHUNKS], F32)
+            nc.scalar.activation(
+                out=parts_copy[:], in_=k_sumsq_parts[:, i, :], func=ACT.Identity, accum_out=k_sumsq[:, i : i + 1]
+            )
+            nc.scalar.activation(
+                out=k_rstd[:, i : i + 1],
+                in_=k_sumsq[:, i : i + 1],
+                func=ACT.Abs_reciprocal_sqrt,
+                scale=1.0 / D,
+                bias=eps[:],
+            )
+            nc.vector.scalar_tensor_tensor(
+                out=k_tile[:], in0=k_tile[:], scalar=k_rstd[:, i : i + 1], in1=kn_bc[:], op0=ALU.mult, op1=ALU.mult
+            )
+            nc.sync.dma_start(out=out_rows[i * P : (i + 1) * P, :], in_=k_tile[:])
+
+        load_tokens(0)
+        nc.scalar.dma_start(out=fn_bc[:], in_=fn_w.partition_broadcast(P))
+        load_tokens(1)
+        prepare_tokens(0)
+        prepare_tokens(1)
+        prepare_chunk(0)
+        for i in range(2, EARLY):
+            load_tokens(i)
+            prepare_tokens(i)
+        nc.sync.dma_start(out=bias_bc[:], in_=Wk_b.partition_broadcast(P))
+        for j in range(CHUNKS):
+            if j + 1 < CHUNKS:
+                prepare_chunk(j + 1)
+            load_tokens(EARLY + j)
+            prepare_tokens(EARLY + j)
+            for i in range(EARLY):
+                multiply(i, j)
+        nc.sync.dma_start(out=kn_bc[:], in_=kn_w.partition_broadcast(P))
+        for i in range(EARLY, TOKEN_TILES):
+            for j in range(CHUNKS):
+                multiply(i, j)
+            finish(i - EARLY)
+        for i in range(EARLY, TOKEN_TILES):
+            finish(i)

@@ -47,21 +47,38 @@ def tile_crossattention_pa_kernel(tc, features, fn_w, Wk_w, Wk_b, kn_w, out):
         eps = const.tile([P, 1], F32)
         nc.vector.memset(eps[:], EPS)
         warm = const.tile([P, 1], F32)
-        nc.scalar.activation(out=warm[:], in_=eps[:], func=ACT.Abs_reciprocal_sqrt)
+        nc.scalar.activation(out=warm[:], in_=eps[:], func=ACT.Sqrt)
         ident = const.tile([P, P], F32)
         make_identity(nc, ident[:])
-        fn_bc = const.tile([P, D], BF16)
-        bias_bc = const.tile([P, D], BF16)
-        kn_bc = const.tile([P, D], BF16)
+
+        vec_rows = const.tile([P, D], BF16)
+        nc.vector.memset(vec_rows[:], 0.0)
+        pick_row = const.tile([P, 3, P], BF16)
+        nc.vector.memset(pick_row[:], 0.0)
+        spread = []
+        for v, vec in enumerate((fn_w, Wk_b, kn_w)):
+            nc.vector.memset(pick_row[32 * v : 32 * v + 1, v, :], 1.0)
+            nc.scalar.dma_start(out=vec_rows[32 * v : 32 * v + 1, :], in_=vec.unsqueeze(0))
+            spread.append(const.tile([P, D], BF16, name="spread%d" % v))
+        fn_bc, bias_bc, kn_bc = spread
+
+        def spread_vector(v):
+            for j in range(CHUNKS):
+                cols = slice(j * CHUNK, (j + 1) * CHUNK)
+                bank = psum_mx.tile([P, CHUNK], F32, name="acc")
+                nc.tensor.matmul(out=bank[:], lhsT=pick_row[:, v, :], rhs=vec_rows[:, cols], start=True, stop=True)
+                nc.vector.tensor_copy(out=spread[v][:, cols], in_=bank[:])
 
         x_codes = keep.tile([P, TOKEN_TILES, PASSES * P], U32, align_bytes=64)
         x_scales = keep.tile([P, TOKEN_TILES, PASSES * P], U8, align_bytes=64)
         w_codes = keep.tile([P, CHUNKS, PASSES * CHUNK], U32, align_bytes=64)
         w_scales = keep.tile([P, CHUNKS, PASSES * CHUNK], U8, align_bytes=64)
         x_sumsq = keep.tile([P, TOKEN_TILES], F32)
+        x_rms = keep.tile([P, TOKEN_TILES], F32)
         x_rstd = keep.tile([P, TOKEN_TILES], F32)
         k_sumsq_parts = keep.tile([P, TOKEN_TILES, CHUNKS], F32)
         k_sumsq = keep.tile([P, TOKEN_TILES], F32)
+        k_rms = keep.tile([P, TOKEN_TILES], F32)
         k_rstd = keep.tile([P, TOKEN_TILES], F32)
         x_raw = {}
         k_tiles = {}
@@ -88,12 +105,9 @@ def tile_crossattention_pa_kernel(tc, features, fn_w, Wk_w, Wk_b, kn_w, out):
                 out=squares[:], in_=x_raw[i][:], func=ACT.Square, accum_out=x_sumsq[:, i : i + 1]
             )
             nc.scalar.activation(
-                out=x_rstd[:, i : i + 1],
-                in_=x_sumsq[:, i : i + 1],
-                func=ACT.Abs_reciprocal_sqrt,
-                scale=1.0 / D,
-                bias=eps[:],
+                out=x_rms[:, i : i + 1], in_=x_sumsq[:, i : i + 1], func=ACT.Sqrt, scale=1.0 / D, bias=eps[:]
             )
+            nc.vector.reciprocal(out=x_rstd[:, i : i + 1], in_=x_rms[:, i : i + 1])
             x_n = work.tile([P, D], BF16)
             nc.vector.scalar_tensor_tensor(
                 out=x_n[:], in0=x_raw[i][:], scalar=x_rstd[:, i : i + 1], in1=fn_bc[:], op0=ALU.mult, op1=ALU.mult
@@ -155,27 +169,25 @@ def tile_crossattention_pa_kernel(tc, features, fn_w, Wk_w, Wk_b, kn_w, out):
                 out=parts_copy[:], in_=k_sumsq_parts[:, i, :], func=ACT.Identity, accum_out=k_sumsq[:, i : i + 1]
             )
             nc.scalar.activation(
-                out=k_rstd[:, i : i + 1],
-                in_=k_sumsq[:, i : i + 1],
-                func=ACT.Abs_reciprocal_sqrt,
-                scale=1.0 / D,
-                bias=eps[:],
+                out=k_rms[:, i : i + 1], in_=k_sumsq[:, i : i + 1], func=ACT.Sqrt, scale=1.0 / D, bias=eps[:]
             )
+            nc.vector.reciprocal(out=k_rstd[:, i : i + 1], in_=k_rms[:, i : i + 1])
             nc.vector.scalar_tensor_tensor(
                 out=k_tile[:], in0=k_tile[:], scalar=k_rstd[:, i : i + 1], in1=kn_bc[:], op0=ALU.mult, op1=ALU.mult
             )
             nc.sync.dma_start(out=out_rows[i * P : (i + 1) * P, :], in_=k_tile[:])
 
         load_tokens(0)
-        nc.scalar.dma_start(out=fn_bc[:], in_=fn_w.partition_broadcast(P))
         load_tokens(1)
+        spread_vector(0)
         prepare_tokens(0)
         prepare_tokens(1)
+        spread_vector(1)
+        spread_vector(2)
         prepare_chunk(0)
         for i in range(2, EARLY):
             load_tokens(i)
             prepare_tokens(i)
-        nc.sync.dma_start(out=bias_bc[:], in_=Wk_b.partition_broadcast(P))
         for j in range(CHUNKS):
             if j + 1 < CHUNKS:
                 prepare_chunk(j + 1)
@@ -183,7 +195,6 @@ def tile_crossattention_pa_kernel(tc, features, fn_w, Wk_w, Wk_b, kn_w, out):
             prepare_tokens(EARLY + j)
             for i in range(EARLY):
                 multiply(i, j)
-        nc.sync.dma_start(out=kn_bc[:], in_=kn_w.partition_broadcast(P))
         for i in range(EARLY, TOKEN_TILES):
             for j in range(CHUNKS):
                 multiply(i, j)

@@ -7,6 +7,7 @@ F32 = mybir.dt.float32
 BF16 = mybir.dt.bfloat16
 U32 = mybir.dt.uint32
 U8 = mybir.dt.uint8
+I32 = mybir.dt.int32
 FP8X4 = mybir.dt.float8_e4m3fn_x4
 ALU = mybir.AluOpType
 ACT = mybir.ActivationFunctionType
@@ -24,7 +25,6 @@ CHUNKS = D // CHUNK
 W_TILES_PER_CHUNK = CHUNK // P
 TOKEN_TILES = TOKENS // P
 EARLY = 4
-assert TOKEN_TILES - EARLY == CHUNKS
 
 FLOPS = 2 * TOKENS * D * D
 
@@ -41,8 +41,7 @@ def tile_crossattention_pa_kernel(tc, features, fn_w, Wk_w, Wk_b, kn_w, out):
         w_in = ctx.enter_context(tc.tile_pool(name="w_in", bufs=6))
         work = ctx.enter_context(tc.tile_pool(name="work", bufs=2))
         k_pool = ctx.enter_context(tc.tile_pool(name="k_pool", bufs=EARLY + 2))
-        psum_t = ctx.enter_context(tc.psum_pool(name="psum_t", bufs=4))
-        psum_mx = ctx.enter_context(tc.psum_pool(name="psum_mx", bufs=4))
+        psum = ctx.enter_context(tc.psum_pool(name="psum", bufs=8))
 
         eps = const.tile([P, 1], F32)
         nc.vector.memset(eps[:], EPS)
@@ -51,23 +50,23 @@ def tile_crossattention_pa_kernel(tc, features, fn_w, Wk_w, Wk_b, kn_w, out):
         ident = const.tile([P, P], F32)
         make_identity(nc, ident[:])
 
-        vec_rows = const.tile([P, D], BF16)
-        nc.vector.memset(vec_rows[:], 0.0)
-        pick_row = const.tile([P, 3, P], BF16)
-        nc.vector.memset(pick_row[:], 0.0)
-        spread = []
-        for v, vec in enumerate((fn_w, Wk_b, kn_w)):
-            nc.vector.memset(pick_row[32 * v : 32 * v + 1, v, :], 1.0)
-            nc.scalar.dma_start(out=vec_rows[32 * v : 32 * v + 1, :], in_=vec.unsqueeze(0))
-            spread.append(const.tile([P, D], BF16, name="spread%d" % v))
-        fn_bc, bias_bc, kn_bc = spread
+        fn_bc = const.tile([P, D], BF16)
+        bias_bc = const.tile([P, D], BF16)
+        kn_bc = const.tile([P, D], BF16)
+        fn_loaded = const.tile([1, D], BF16)
+        nc.sync.dma_start(out=fn_loaded[:], in_=fn_w.unsqueeze(0))
+        fn_row = const.tile([P, D], BF16)
+        nc.vector.memset(fn_row[:].bitcast(I32), 0)
+        nc.vector.tensor_copy(out=fn_row[0:1, :], in_=fn_loaded[:])
+        ones = const.tile([P, P], BF16)
+        nc.vector.memset(ones[:], 1.0)
 
-        def spread_vector(v):
+        def spread_fn_w():
             for j in range(CHUNKS):
                 cols = slice(j * CHUNK, (j + 1) * CHUNK)
-                bank = psum_mx.tile([P, CHUNK], F32, name="acc")
-                nc.tensor.matmul(out=bank[:], lhsT=pick_row[:, v, :], rhs=vec_rows[:, cols], start=True, stop=True)
-                nc.vector.tensor_copy(out=spread[v][:, cols], in_=bank[:])
+                bank = psum.tile([P, CHUNK], F32, tag="bank")
+                nc.tensor.matmul(out=bank[:], lhsT=ones[:], rhs=fn_row[:, cols], start=True, stop=True)
+                nc.vector.tensor_copy(out=fn_bc[:, cols], in_=bank[:])
 
         x_codes = keep.tile([P, TOKEN_TILES, PASSES * P], U32, align_bytes=64)
         x_scales = keep.tile([P, TOKEN_TILES, PASSES * P], U8, align_bytes=64)
@@ -89,7 +88,7 @@ def tile_crossattention_pa_kernel(tc, features, fn_w, Wk_w, Wk_b, kn_w, out):
 
         def k_onto_partitions(rows_words, grouped_words, copy):
             for half in range(2):
-                bank = psum_t.tile([P, 2, 2, P], F32)
+                bank = psum.tile([P, 2, 2, P], F32, tag="bank")
                 for c2 in range(2):
                     for u in range(2):
                         first = ((2 * half + c2) * 2 + u) * P
@@ -138,9 +137,9 @@ def tile_crossattention_pa_kernel(tc, features, fn_w, Wk_w, Wk_b, kn_w, out):
                 )
 
         def multiply(i, j):
-            if j == 0:
+            if i not in k_tiles:
                 k_tiles[i] = k_pool.tile([P, D], F32, name="k_tile")
-            acc = psum_mx.tile([P, CHUNK], F32)
+            acc = psum.tile([P, CHUNK], F32, tag="bank")
             for c in range(PASSES):
                 nc.tensor.matmul_mx(
                     out=acc[:],
@@ -177,27 +176,28 @@ def tile_crossattention_pa_kernel(tc, features, fn_w, Wk_w, Wk_b, kn_w, out):
             )
             nc.sync.dma_start(out=out_rows[i * P : (i + 1) * P, :], in_=k_tile[:])
 
-        load_tokens(0)
-        load_tokens(1)
-        spread_vector(0)
-        prepare_tokens(0)
-        prepare_tokens(1)
-        spread_vector(1)
-        spread_vector(2)
-        prepare_chunk(0)
-        for i in range(2, EARLY):
-            load_tokens(i)
-            prepare_tokens(i)
-        for j in range(CHUNKS):
-            if j + 1 < CHUNKS:
-                prepare_chunk(j + 1)
-            load_tokens(EARLY + j)
-            prepare_tokens(EARLY + j)
-            for i in range(EARLY):
-                multiply(i, j)
-        for i in range(EARLY, TOKEN_TILES):
-            for j in range(CHUNKS):
-                multiply(i, j)
-            finish(i - EARLY)
-        for i in range(EARLY, TOKEN_TILES):
+        def prepare_round(r):
+            load_tokens(r)
+            prepare_tokens(r)
+            if r < CHUNKS:
+                prepare_chunk(r)
+
+        spread_fn_w()
+        prepare_round(0)
+        nc.sync.dma_start(out=bias_bc[:], in_=Wk_b.partition_broadcast(P))
+        for r in range(TOKEN_TILES):
+            if r + 1 < TOKEN_TILES:
+                prepare_round(r + 1)
+            if r == CHUNKS:
+                nc.sync.dma_start(out=kn_bc[:], in_=kn_w.partition_broadcast(P))
+            if r < CHUNKS:
+                for j in range(r):
+                    multiply(r, j)
+                for i in range(r + 1):
+                    multiply(i, r)
+            else:
+                for j in range(CHUNKS):
+                    multiply(r, j)
+                finish(r - CHUNKS)
+        for i in range(TOKEN_TILES - CHUNKS, TOKEN_TILES):
             finish(i)

@@ -25,6 +25,7 @@ CHUNKS = D // CHUNK
 W_TILES_PER_CHUNK = CHUNK // P
 TOKEN_TILES = TOKENS // P
 EARLY = 4
+POOL_TILES = 3
 
 FLOPS = 2 * TOKENS * D * D
 
@@ -67,6 +68,25 @@ def tile_crossattention_pa_kernel(tc, features, fn_w, Wk_w, Wk_b, kn_w, out):
                 bank = psum.tile([P, CHUNK], F32, tag="bank")
                 nc.tensor.matmul(out=bank[:], lhsT=ones[:], rhs=fn_row[:, cols], start=True, stop=True)
                 nc.vector.tensor_copy(out=fn_bc[:, cols], in_=bank[:])
+
+        kn_loaded = const.tile([1, D], BF16)
+        nc.sync.dma_start(out=kn_loaded[:], in_=kn_w.unsqueeze(0))
+        kn_banks = []
+
+        def spread_kn_w():
+            nc.vector.tensor_copy(out=fn_row[0:1, :], in_=kn_loaded[:])
+            for half in range(2):
+                kn_bank = psum.tile([P, 2 * CHUNK], BF16, tag="bank", name="kn_bank%d" % half)
+                for q in range(2):
+                    first = (2 * half + q) * CHUNK
+                    nc.tensor.matmul(
+                        out=kn_bank[:, q * CHUNK : (q + 1) * CHUNK],
+                        lhsT=ones[:],
+                        rhs=fn_row[:, first : first + CHUNK],
+                        start=True,
+                        stop=True,
+                    )
+                kn_banks.append(kn_bank)
 
         x_codes = keep.tile([P, TOKEN_TILES, PASSES * P], U32, align_bytes=64)
         x_scales = keep.tile([P, TOKEN_TILES, PASSES * P], U8, align_bytes=64)
@@ -171,9 +191,31 @@ def tile_crossattention_pa_kernel(tc, features, fn_w, Wk_w, Wk_b, kn_w, out):
                 out=k_rms[:, i : i + 1], in_=k_sumsq[:, i : i + 1], func=ACT.Sqrt, scale=1.0 / D, bias=eps[:]
             )
             nc.vector.reciprocal(out=k_rstd[:, i : i + 1], in_=k_rms[:, i : i + 1])
-            nc.vector.scalar_tensor_tensor(
-                out=k_tile[:], in0=k_tile[:], scalar=k_rstd[:, i : i + 1], in1=kn_bc[:], op0=ALU.mult, op1=ALU.mult
-            )
+            if i < POOL_TILES:
+                for j in range(CHUNKS):
+                    cols = slice(j * CHUNK, (j + 1) * CHUNK)
+                    nc.gpsimd.tensor_tensor(out=k_tile[:, cols], in0=k_tile[:, cols], in1=kn_bc[:, cols], op=ALU.mult)
+                for j in range(CHUNKS):
+                    cols = slice(j * CHUNK, (j + 1) * CHUNK)
+                    nc.gpsimd.tensor_scalar(
+                        out=k_tile[:, cols],
+                        in0=k_tile[:, cols],
+                        scalar1=k_rstd[:, i : i + 1],
+                        scalar2=0.0,
+                        op0=ALU.mult,
+                        op1=ALU.add,
+                    )
+            else:
+                for half in range(2):
+                    cols = slice(half * 2 * CHUNK, (half + 1) * 2 * CHUNK)
+                    nc.vector.scalar_tensor_tensor(
+                        out=k_tile[:, cols],
+                        in0=k_tile[:, cols],
+                        scalar=k_rstd[:, i : i + 1],
+                        in1=kn_banks[half][:],
+                        op0=ALU.mult,
+                        op1=ALU.mult,
+                    )
             nc.sync.dma_start(out=out_rows[i * P : (i + 1) * P, :], in_=k_tile[:])
 
         def prepare_round(r):
@@ -190,6 +232,7 @@ def tile_crossattention_pa_kernel(tc, features, fn_w, Wk_w, Wk_b, kn_w, out):
                 prepare_round(r + 1)
             if r == CHUNKS:
                 nc.sync.dma_start(out=kn_bc[:], in_=kn_w.partition_broadcast(P))
+                spread_kn_w()
             if r < CHUNKS:
                 for j in range(r):
                     multiply(r, j)

from contextlib import ExitStack

import concourse.mybir as mybir
from concourse.masks import make_identity

F32 = mybir.dt.float32
BF16 = mybir.dt.bfloat16
U32 = mybir.dt.uint32
U8 = mybir.dt.uint8
I32 = mybir.dt.int32
FP8X4 = mybir.dt.float8_e4m3fn_x4
ALU = mybir.AluOpType
ACT = mybir.ActivationFunctionType

P = 128
TOKENS = 1024
D = 2048
EPS = 1e-6
PACK = 4
K_PASS = P * PACK
PASSES = D // K_PASS
WORDS = D // 2
CHUNK = 512
CHUNKS = D // CHUNK
W_TILES_PER_CHUNK = CHUNK // P
TOKEN_TILES = TOKENS // P
EARLY = 4
POOL_TILES = 3

FLOPS = 2 * TOKENS * D * D


def tile_crossattention_pa_kernel(tc, features, fn_w, Wk_w, Wk_b, kn_w, out):
    nc = tc.nc
    x_rows = features.flatten_outer_dims()
    out_rows = out.flatten_outer_dims()

    with ExitStack() as ctx:
        const = ctx.enter_context(tc.tile_pool(name="const", bufs=1))
        keep = ctx.enter_context(tc.tile_pool(name="keep", bufs=1))
        x_in = ctx.enter_context(tc.tile_pool(name="x_in", bufs=4))
        w_in = ctx.enter_context(tc.tile_pool(name="w_in", bufs=6))
        work = ctx.enter_context(tc.tile_pool(name="work", bufs=2))
        k_pool = ctx.enter_context(tc.tile_pool(name="k_pool", bufs=EARLY + 2))
        psum = ctx.enter_context(tc.psum_pool(name="psum", bufs=8))

        eps = const.tile([P, 1], F32)
        nc.vector.memset(eps[:], EPS)
        warm = const.tile([P, 1], F32)
        nc.scalar.activation(out=warm[:], in_=eps[:], func=ACT.Sqrt)
        ident = const.tile([P, P], F32)
        make_identity(nc, ident[:])

        fn_bc = const.tile([P, D], BF16)
        bias_bc = const.tile([P, D], BF16)
        kn_bc = const.tile([P, D], BF16)
        fn_loaded = const.tile([1, D], BF16)
        nc.sync.dma_start(out=fn_loaded[:], in_=fn_w.unsqueeze(0))
        fn_row = const.tile([P, D], BF16)
        nc.vector.memset(fn_row[:].bitcast(I32), 0)
        nc.vector.tensor_copy(out=fn_row[0:1, :], in_=fn_loaded[:])
        ones = const.tile([P, P], BF16)
        nc.vector.memset(ones[:], 1.0)

        def spread_fn_w():
            for j in range(CHUNKS):
                cols = slice(j * CHUNK, (j + 1) * CHUNK)
                bank = psum.tile([P, CHUNK], F32, tag="bank")
                nc.tensor.matmul(out=bank[:], lhsT=ones[:], rhs=fn_row[:, cols], start=True, stop=True)
                nc.vector.tensor_copy(out=fn_bc[:, cols], in_=bank[:])

        kn_loaded = const.tile([1, D], BF16)
        nc.sync.dma_start(out=kn_loaded[:], in_=kn_w.unsqueeze(0))
        kn_banks = []

        def spread_kn_w():
            nc.vector.tensor_copy(out=fn_row[0:1, :], in_=kn_loaded[:])
            for half in range(2):
                kn_bank = psum.tile([P, 2 * CHUNK], BF16, tag="bank", name="kn_bank%d" % half)
                for q in range(2):
                    first = (2 * half + q) * CHUNK
                    nc.tensor.matmul(
                        out=kn_bank[:, q * CHUNK : (q + 1) * CHUNK],
                        lhsT=ones[:],
                        rhs=fn_row[:, first : first + CHUNK],
                        start=True,
                        stop=True,
                    )
                kn_banks.append(kn_bank)

        x_codes = keep.tile([P, TOKEN_TILES, PASSES * P], U32, align_bytes=64)
        x_scales = keep.tile([P, TOKEN_TILES, PASSES * P], U8, align_bytes=64)
        w_codes = keep.tile([P, CHUNKS, PASSES * CHUNK], U32, align_bytes=64)
        w_scales = keep.tile([P, CHUNKS, PASSES * CHUNK], U8, align_bytes=64)
        x_sumsq = keep.tile([P, TOKEN_TILES], F32)
        x_rms = keep.tile([P, TOKEN_TILES], F32)
        x_rstd = keep.tile([P, TOKEN_TILES], F32)
        k_sumsq_parts = keep.tile([P, TOKEN_TILES, CHUNKS], F32)
        k_sumsq = keep.tile([P, TOKEN_TILES], F32)
        k_rms = keep.tile([P, TOKEN_TILES], F32)
        k_rstd = keep.tile([P, TOKEN_TILES], F32)
        x_raw = {}
        k_tiles = {}

        def load_tokens(i):
            x_raw[i] = x_in.tile([P, D], BF16, name="x_raw")
            nc.sync.dma_start(out=x_raw[i][:], in_=x_rows[i * P : (i + 1) * P, :])

        def k_onto_partitions(rows_words, grouped_words, copy):
            for half in range(2):
                bank = psum.tile([P, 2, 2, P], F32, tag="bank")
                for c2 in range(2):
                    for u in range(2):
                        first = ((2 * half + c2) * 2 + u) * P
                        nc.tensor.transpose(bank[:, c2, u, :], rows_words[:, first : first + P], ident[:])
                copy(
                    out=grouped_words[:, 2 * half : 2 * half + 2, :, :],
                    in_=bank[:].rearrange("p c u r -> p c r u"),
                )

        def prepare_tokens(i):
            squares = work.tile([P, D], BF16)
            nc.scalar.activation(
                out=squares[:], in_=x_raw[i][:], func=ACT.Square, accum_out=x_sumsq[:, i : i + 1]
            )
            nc.scalar.activation(
                out=x_rms[:, i : i + 1], in_=x_sumsq[:, i : i + 1], func=ACT.Sqrt, scale=1.0 / D, bias=eps[:]
            )
            nc.vector.reciprocal(out=x_rstd[:, i : i + 1], in_=x_rms[:, i : i + 1])
            x_n = work.tile([P, D], BF16)
            nc.vector.scalar_tensor_tensor(
                out=x_n[:], in0=x_raw[i][:], scalar=x_rstd[:, i : i + 1], in1=fn_bc[:], op0=ALU.mult, op1=ALU.mult
            )
            x_grouped = work.tile([P, D], BF16, align_bytes=64)
            k_onto_partitions(
                x_n[:].bitcast(F32),
                x_grouped[:].bitcast(F32).rearrange("p (c r u) -> p c r u", c=PASSES, r=P, u=2),
                nc.vector.tensor_copy if i < EARLY else nc.scalar.copy,
            )
            nc.vector.quantize_mx(out=x_codes[:, i, :].bitcast(FP8X4), scales=x_scales[:, i, :], in_=x_grouped[:])

        def prepare_chunk(j):
            w_grouped = work.tile([P, PASSES * CHUNK * PACK], BF16, align_bytes=64)
            grouped_words = w_grouped[:].bitcast(F32).rearrange(
                "p (c n r u) -> p c n r u", c=PASSES, n=W_TILES_PER_CHUNK, r=P, u=2
            )
            for n in range(W_TILES_PER_CHUNK):
                first_row = j * CHUNK + n * P
                w_raw = w_in.tile([P, D], BF16)
                nc.sync.dma_start(out=w_raw[:], in_=Wk_w[first_row : first_row + P, :])
                k_onto_partitions(w_raw[:].bitcast(F32), grouped_words[:, :, n, :, :], nc.scalar.copy)
            for c in range(PASSES):
                nc.vector.quantize_mx(
                    out=w_codes[:, j, c * CHUNK : (c + 1) * CHUNK].bitcast(FP8X4),
                    scales=w_scales[:, j, c * CHUNK : (c + 1) * CHUNK],
                    in_=w_grouped[:, c * CHUNK * PACK : (c + 1) * CHUNK * PACK],
                )

        def multiply(i, j):
            if i not in k_tiles:
                k_tiles[i] = k_pool.tile([P, D], F32, name="k_tile")
            acc = psum.tile([P, CHUNK], F32, tag="bank")
            for c in range(PASSES):
                nc.tensor.matmul_mx(
                    out=acc[:],
                    lhsT=x_codes[:, i, c * P : (c + 1) * P].bitcast(FP8X4),
                    lhsT_scale=x_scales[:, i, c * P : (c + 1) * P],
                    rhs=w_codes[:, j, c * CHUNK : (c + 1) * CHUNK].bitcast(FP8X4),
                    rhs_scale=w_scales[:, j, c * CHUNK : (c + 1) * CHUNK],
                    start=(c == 0),
                    stop=(c == PASSES - 1),
                )
            cols = slice(j * CHUNK, (j + 1) * CHUNK)
            nc.vector.tensor_tensor(out=k_tiles[i][:, cols], in0=acc[:], in1=bias_bc[:, cols], op=ALU.add)

        def finish(i):
            k_tile = k_tiles[i]
            for j in range(CHUNKS):
                k_squares = work.tile([P, CHUNK], BF16)
                nc.scalar.activation(
                    out=k_squares[:],
                    in_=k_tile[:, j * CHUNK : (j + 1) * CHUNK],
                    func=ACT.Square,
                    accum_out=k_sumsq_parts[:, i, j : j + 1],
                )
            parts_copy = work.tile([P, CHUNKS], F32)
            nc.scalar.activation(
                out=parts_copy[:], in_=k_sumsq_parts[:, i, :], func=ACT.Identity, accum_out=k_sumsq[:, i : i + 1]
            )
            nc.scalar.activation(
                out=k_rms[:, i : i + 1], in_=k_sumsq[:, i : i + 1], func=ACT.Sqrt, scale=1.0 / D, bias=eps[:]
            )
            nc.vector.reciprocal(out=k_rstd[:, i : i + 1], in_=k_rms[:, i : i + 1])
            if i < POOL_TILES:
                for j in range(CHUNKS):
                    cols = slice(j * CHUNK, (j + 1) * CHUNK)
                    nc.gpsimd.tensor_tensor(out=k_tile[:, cols], in0=k_tile[:, cols], in1=kn_bc[:, cols], op=ALU.mult)
                for j in range(CHUNKS):
                    cols = slice(j * CHUNK, (j + 1) * CHUNK)
                    nc.gpsimd.tensor_scalar(
                        out=k_tile[:, cols],
                        in0=k_tile[:, cols],
                        scalar1=k_rstd[:, i : i + 1],
                        scalar2=0.0,
                        op0=ALU.mult,
                        op1=ALU.add,
                    )
            else:
                for half in range(2):
                    cols = slice(half * 2 * CHUNK, (half + 1) * 2 * CHUNK)
                    nc.vector.scalar_tensor_tensor(
                        out=k_tile[:, cols],
                        in0=k_tile[:, cols],
                        scalar=k_rstd[:, i : i + 1],
                        in1=kn_banks[half][:],
                        op0=ALU.mult,
                        op1=ALU.mult,
                    )
            nc.sync.dma_start(out=out_rows[i * P : (i + 1) * P, :], in_=k_tile[:])

        def prepare_round(r):
            load_tokens(r)
            prepare_tokens(r)
            if r < CHUNKS:
                prepare_chunk(r)

        spread_fn_w()
        prepare_round(0)
        nc.sync.dma_start(out=bias_bc[:], in_=Wk_b.partition_broadcast(P))
        for r in range(TOKEN_TILES):
            if r + 1 < TOKEN_TILES:
                prepare_round(r + 1)
            if r == CHUNKS:
                nc.sync.dma_start(out=kn_bc[:], in_=kn_w.partition_broadcast(P))
                spread_kn_w()
            if r < CHUNKS:
                for j in range(r):
                    multiply(r, j)
                for i in range(r + 1):
                    multiply(i, r)
            else:
                for j in range(CHUNKS):
                    multiply(r, j)
                finish(r - CHUNKS)
        for i in range(TOKEN_TILES - CHUNKS, TOKEN_TILES):
            finish(i)
